import numpy as np
import ml_dtypes


def mxq(x, axis, fmt="e4m3"):
    dtype, down = {"e4m3": (ml_dtypes.float8_e4m3fn, 7), "e5m2": (ml_dtypes.float8_e5m2, 14)}[fmt]
    v = np.moveaxis(np.asarray(x, np.float32).astype(ml_dtypes.bfloat16).astype(np.float64), axis, -1)
    blocks = v.reshape(v.shape[:-1] + (-1, 32))
    amax = np.abs(blocks).max(-1, keepdims=True)
    byte = np.maximum(np.where(amax > 0, np.frexp(amax)[1] - 1 + 127, 0) - down, 1)
    scale = np.exp2(byte - 127.0)
    codes = (blocks / scale).astype(np.float32).astype(dtype).astype(np.float64)
    return np.moveaxis((codes * scale).reshape(v.shape), -1, axis)


WIDE = False


def mx_kscale(k):
    if not WIDE:
        return np.ones(k)
    levels = np.array([10, -10, 5, -5, 0])
    a = np.random.permutation(np.resize(levels, k // 512 * 4)).reshape(k // 512, 4)
    idx = np.arange(k)
    return np.exp2(a[idx // 512, idx % 128 // 32])


BF16 = ml_dtypes.bfloat16


def bf(x):
    return np.asarray(x, np.float32).astype(BF16)


def f64(x):
    return np.asarray(x).astype(np.float64)


E2M1 = np.array([0.0, 0.5, 1.0, 1.5, 2.0, 3.0, 4.0, 6.0, -0.0, -0.5, -1.0, -1.5, -2.0, -3.0, -4.0, -6.0])


def pack_weight(w, fmt):
    k, n = w.shape
    w = f64(bf(w)).reshape(k // 32, 32, n)
    amax = np.abs(w).max(1)
    if fmt == "e4m3":
        byte = np.frexp(amax)[1] - 1 + 127 - 7
    else:
        mant, ex = np.frexp(amax / 6.0)
        byte = np.where(mant > 0.5, ex, ex - 1) + 127
    byte = np.clip(np.where(amax > 0, byte, 1), 1, 254)
    scaled = (w * np.exp2(127.0 - byte)[:, None, :]).reshape(k, n).astype(np.float32)
    by_word = np.ascontiguousarray(scaled.reshape(k // 512, 128, 4, n).transpose(0, 1, 3, 2))
    if fmt == "e4m3":
        words = by_word.astype(ml_dtypes.float8_e4m3fn).view(np.uint8)
    else:
        c = by_word.astype(ml_dtypes.float4_e2m1fn).view(np.uint8) & 0xF
        words = c[..., 0::2] | (c[..., 1::2] << 4)
    return np.ascontiguousarray(words), np.ascontiguousarray(byte.astype(np.uint8).reshape(k // 512, 16, n))


def unpack_weight(words, scales, fmt):
    g, p, n, _ = words.shape
    if fmt == "e4m3":
        vals = np.ascontiguousarray(words).view(ml_dtypes.float8_e4m3fn).astype(np.float64)
    else:
        nib = np.empty((g, p, n, 4), np.uint8)
        nib[..., 0::2] = words & 0xF
        nib[..., 1::2] = words >> 4
        vals = E2M1[nib]
    vals = vals * np.repeat(np.exp2(scales.astype(np.float64) - 127.0), 8, axis=1)[..., None]
    return vals.transpose(0, 1, 3, 2).reshape(g * 512, n)

def pack4(w):
    words, scales = pack_weight(w, "e2m1")
    return words.reshape(words.shape[0], 128, -1), scales


def unpack4(words, scales):
    return unpack_weight(words.reshape(words.shape[0], 128, -1, 2), scales, "e2m1")


B, D, E, H, W, SHIFT = 4, 512, 512, 16, 16, 5
EPS = 1e-5


def erf(v):
    a = np.clip(v, -6.0, 6.0)
    a2 = 2.0 * a * a
    term = a.copy()
    tot = a.copy()
    for n in range(120):
        term = term * a2 / (2 * n + 3)
        tot = tot + term
    return 2.0 / np.sqrt(np.pi) * np.exp(-a * a) * tot


def gelu(v):
    return 0.5 * v * (1.0 + erf(v / np.sqrt(2.0)))


def conv1x1(x, w, b):
    n, c, hh, ww = x.shape
    y = w @ mxq(x.reshape(n, c, hh * ww), 1, "e4m3")
    return y.reshape(n, -1, hh, ww) + b[None, :, None, None]


def group_norm1(x, gamma, beta):
    m = x.mean(axis=(1, 2, 3), keepdims=True)
    v = x.var(axis=(1, 2, 3), keepdims=True)
    xh = (x - m) / np.sqrt(v + EPS)
    return xh * gamma[None, :, None, None] + beta[None, :, None, None]


def setup_inputs():
    s = mx_kscale(D)
    x = bf(np.random.standard_normal((B, D, H, W)) * s[None, :, None, None])
    w1 = np.random.standard_normal((E, D)) / np.sqrt(D) / s[None, :]
    w1_words, w1_scales = pack4(np.ascontiguousarray(w1.T))
    b1 = bf(np.random.standard_normal(E) * 0.3)
    g1 = bf(1.0 + 0.1 * np.random.standard_normal(E))
    be1 = bf(0.2 * np.random.standard_normal(E))
    return {"x": x,
            "w1_words": w1_words,
            "w1_scales": w1_scales,
            "b1": b1,
            "g1": g1,
            "be1": be1}


def reference(x, w1_words, w1_scales, b1, g1, be1):
    y = conv1x1(f64(x), unpack4(w1_words, w1_scales).T, f64(b1))
    return gelu(group_norm1(y, f64(g1), f64(be1)))

@@ -1,0 +1,225 @@
+from contextlib import ExitStack
+
+import concourse.mybir as mybir
+from concourse.masks import make_identity
+
+F32 = mybir.dt.float32
+BF16 = mybir.dt.bfloat16
+I32 = mybir.dt.int32
+U32 = mybir.dt.uint32
+U8 = mybir.dt.uint8
+FP8X4 = mybir.dt.float8_e4m3fn_x4
+FP4X4 = mybir.dt.float4_e2m1fn_x4
+ALU = mybir.AluOpType
+ACT = mybir.ActivationFunctionType
+
+P = 128
+PACK = 4
+SAMPLES = 4
+CHANNELS = 512
+PIX = 256
+TILES = CHANNELS // P
+HALVES = 2
+EPS = 1e-5
+Y_BANKS = 7
+
+FLOPS = 2 * SAMPLES * PIX * CHANNELS * CHANNELS
+
+
+def tile_axialshift_pa_s_kernel(tc, x, w1_words, w1_scales, b1, g1, be1, out):
+    nc = tc.nc
+    with ExitStack() as ctx:
+        keep = ctx.enter_context(tc.tile_pool(name="keep", bufs=1))
+        y_pool = ctx.enter_context(tc.psum_pool(name="y", bufs=Y_BANKS))
+        small_pool = ctx.enter_context(tc.psum_pool(name="small", bufs=1))
+        ctx.enter_context(tc.manual_schedule())
+
+        w_words = keep.tile([P, 2 * CHANNELS], U8, align_bytes=64)
+        w_plane = keep.tile([P, CHANNELS], U8, align_bytes=64)
+        x_raw = keep.tile([P, SAMPLES, PACK, PIX], BF16)
+        x_grouped = keep.tile([P, SAMPLES, PIX, PACK], BF16, align_bytes=64)
+        x_words = keep.tile([P, SAMPLES, PIX], U32, align_bytes=64)
+        x_plane = keep.tile([P, SAMPLES, PIX], U8, align_bytes=64)
+        result = keep.tile([P, SAMPLES, TILES, PIX], F32)
+
+        vec_rows = keep.tile([P, P], BF16)
+        ident = keep.tile([P, P], BF16)
+        mean_matrix = keep.tile([P, P], F32)
+        minus_half = keep.tile([P, 1], F32)
+        warm = keep.tile([P, 1], F32)
+        bias_eps = keep.tile([P, TILES, 2], F32)
+        bias_gain = keep.tile([P, TILES], F32)
+        gain_offset = keep.tile([P, SAMPLES, 2 * TILES], F32)
+        zero_beta = keep.tile([P, 2 * TILES], F32)
+        stats = keep.tile([P, SAMPLES, HALVES, 2, 3], F32)
+        partial = keep.tile([P, SAMPLES, 4], F32)
+        var_eps = keep.tile([P, SAMPLES], F32)
+        rstd = keep.tile([P, SAMPLES], F32)
+        scale_shift = keep.tile([P, SAMPLES, 2 * TILES], F32)
+
+        nc.vector.memset(w_plane[:].bitcast(I32), 0)
+        nc.vector.memset(minus_half[:], -0.5)
+        nc.vector.memset(mean_matrix[:], 1.0 / P)
+        nc.vector.memset(bias_eps[:], PIX * EPS)
+        nc.vector.memset(zero_beta[:], 0.0)
+        nc.vector.memset(partial[:], 0.0)
+
+        nc.gpsimd.memset(vec_rows[:], 0.0)
+        for row, vec in enumerate((b1, g1, be1)):
+            nc.gpsimd.dma_start(
+                out=vec_rows[TILES * row : TILES * (row + 1), :],
+                in_=vec.rearrange("(t p) -> t p", p=P),
+            )
+        make_identity(nc, ident[:])
+
+        for n in range(SAMPLES):
+            nc.scalar.dma_start(
+                out=x_raw[:, n].rearrange("p j w -> p (j w)"),
+                in_=x[n].rearrange("(p j) h w -> p (j h w)", j=PACK),
+            )
+        nc.sync.dma_start(out=w_words[:].bitcast(I32), in_=w1_words[0].bitcast(I32))
+        for q in range(4):
+            nc.sync.dma_start(
+                out=w_plane[32 * q : 32 * q + 4, :].bitcast(I32),
+                in_=w1_scales[0, 4 * q : 4 * q + 4, :].bitcast(I32),
+            )
+
+        nc.scalar.activation(out=warm[:], in_=minus_half[:], func=ACT.Gelu)
+
+        y_banks = {}
+
+        def regroup(engine_copy, n):
+            engine_copy(
+                out=x_grouped[:, n].rearrange("p (c i) j -> p c j i", i=4),
+                in_=x_raw[:, n].rearrange("p j (c i) -> p c j i", i=4),
+            )
+
+        def quantise(n):
+            nc.vector.quantize_mx(
+                out=x_words[:, n, :].bitcast(FP8X4),
+                scales=x_plane[:, n, :],
+                in_=x_grouped[:, n].rearrange("p w j -> p (w j)"),
+            )
+
+        def multiply(n):
+            for h in range(HALVES):
+                y_bank = y_pool.tile([P, 2, PIX], F32, name="y_bank")
+                y_banks[(n, h)] = y_bank
+                for i in range(2):
+                    t = 2 * h + i
+                    nc.tensor.matmul_mx(
+                        out=y_bank[:, i, :],
+                        lhsT=w_words[:, 2 * P * t : 2 * P * (t + 1)].bitcast(FP4X4),
+                        lhsT_scale=w_plane[:, P * t : P * (t + 1)],
+                        rhs=x_words[:, n, :].bitcast(FP8X4),
+                        rhs_scale=x_plane[:, n, :],
+                        start=True,
+                        stop=True,
+                    )
+
+        def channel_stats(n, h):
+            nc.vector.bn_stats(
+                out=stats[:, n, h].rearrange("p i s -> p (i s)"),
+                in_=y_banks[(n, h)][:].rearrange("p i w -> p w i"),
+            )
+
+        def partition_sums(n):
+            triples = stats[:, n].rearrange("p h i s -> p (h i) s")
+            nc.vector.tensor_tensor(
+                out=triples[:, :, 1:3], in0=triples[:, :, 1:3], in1=bias_eps[:], op=ALU.add
+            )
+            nc.vector.bn_aggr(out=partial[:, n, 0:2], in_=stats[:, n].rearrange("p h i s -> p (h i s)"))
+            nc.vector.scalar_tensor_tensor(
+                out=partial[:, n, 1:2],
+                in0=partial[:, n, 0:1],
+                scalar=partial[:, n, 0:1],
+                in1=partial[:, n, 1:2],
+                op0=ALU.mult,
+                op1=ALU.add,
+            )
+            nc.vector.tensor_scalar(
+                out=partial[:, n, 2:3], in0=partial[:, n, 0:1], scalar1=-1.0, scalar2=None, op0=ALU.mult
+            )
+            nc.tensor.matmul(
+                out=totals[:, n, :], lhsT=mean_matrix[:], rhs=partial[:, n, :], start=True, stop=True
+            )
+
+        def norm_first(n):
+            mean, square, minus_mean = (totals[:, n, c : c + 1] for c in range(3))
+            nc.vector.tensor_scalar(
+                out=var_eps[:, n : n + 1], in0=mean, scalar1=minus_mean, scalar2=square,
+                op0=ALU.mult, op1=ALU.add,
+            )
+            nc.gpsimd.tensor_tensor(
+                out=rstd[:, n : n + 1], in0=var_eps[:, n : n + 1], in1=minus_half[:], op=ALU.pow
+            )
+            nc.vector.scalar_tensor_tensor(
+                out=gain_offset[:, n, TILES:],
+                in0=gain_offset[:, n, 0:TILES],
+                scalar=minus_mean,
+                in1=bias_gain[:],
+                op0=ALU.mult,
+                op1=ALU.add,
+            )
+
+        def norm_second(n):
+            nc.vector.scalar_tensor_tensor(
+                out=scale_shift[:, n, :],
+                in0=gain_offset[:, n, :],
+                scalar=rstd[:, n : n + 1],
+                in1=zero_beta[:],
+                op0=ALU.mult,
+                op1=ALU.add,
+            )
+
+        def gelu_store(n):
+            for t in range(TILES):
+                nc.scalar.activation(
+                    out=result[:, n, t, :],
+                    in_=y_banks[(n, t // 2)][:, t % 2, :],
+                    func=ACT.Gelu,
+                    scale=scale_shift[:, n, t : t + 1],
+                    bias=scale_shift[:, n, TILES + t : TILES + t + 1],
+                )
+                nc.sync.dma_start(
+                    out=out[n, P * t : P * (t + 1)].rearrange("o h w -> o (h w)"),
+                    in_=result[:, n, t, :],
+                )
+
+        def spread_vectors():
+            vec_cols = small_pool.tile([P, P], BF16, tag="small")
+            nc.tensor.transpose(vec_cols[:], vec_rows[:], ident[:])
+            nc.vector.tensor_copy(out=bias_eps[:, :, 0], in_=vec_cols[:, 0:TILES])
+            nc.vector.tensor_copy(
+                out=gain_offset[:, :, 0:TILES],
+                in_=vec_cols[:, TILES : 2 * TILES].unsqueeze(1).to_broadcast([P, SAMPLES, TILES]),
+            )
+            nc.vector.tensor_copy(out=zero_beta[:, TILES:], in_=vec_cols[:, 2 * TILES : 3 * TILES])
+            nc.vector.tensor_tensor(
+                out=bias_gain[:], in0=vec_cols[:, 0:TILES], in1=gain_offset[:, 0, 0:TILES], op=ALU.mult
+            )
+
+        regroup(nc.vector.tensor_copy, 0)
+        for n in range(1, SAMPLES):
+            regroup(nc.scalar.copy, n)
+        quantise(0)
+        multiply(0)
+
+        for n in range(SAMPLES):
+            channel_stats(n, 0)
+            if n + 1 < SAMPLES:
+                quantise(n + 1)
+                multiply(n + 1)
+            channel_stats(n, 1)
+            if n == 0:
+                spread_vectors()
+                totals = small_pool.tile([P, SAMPLES, 4], F32, tag="small")
+            else:
+                norm_first(n - 1)
+            partition_sums(n)
+            if n >= 1:
+                norm_second(n - 1)
+                gelu_store(n - 1)
+        norm_first(SAMPLES - 1)
+        norm_second(SAMPLES - 1)
+        gelu_store(SAMPLES - 1)

@@ -22,6 +22,7 @@ TILES = CHANNELS // P
 HALVES = 2
 EPS = 1e-5
 Y_BANKS = 7
+AHEAD = 2
 
 FLOPS = 2 * SAMPLES * PIX * CHANNELS * CHANNELS
 
@@ -58,31 +59,33 @@ def tile_axialshift_pa_s_kernel(tc, x, w1_words, w1_scales, b1, g1, be1, out):
         scale_shift = keep.tile([P, SAMPLES, 2 * TILES], F32)
 
         nc.vector.memset(w_plane[:].bitcast(I32), 0)
+        nc.vector.memset(vec_rows[:], 0.0)
         nc.vector.memset(minus_half[:], -0.5)
         nc.vector.memset(mean_matrix[:], 1.0 / P)
         nc.vector.memset(bias_eps[:], PIX * EPS)
         nc.vector.memset(zero_beta[:], 0.0)
         nc.vector.memset(partial[:], 0.0)
 
-        nc.gpsimd.memset(vec_rows[:], 0.0)
-        for row, vec in enumerate((b1, g1, be1)):
-            nc.gpsimd.dma_start(
-                out=vec_rows[TILES * row : TILES * (row + 1), :],
-                in_=vec.rearrange("(t p) -> t p", p=P),
-            )
-        make_identity(nc, ident[:])
-
-        for n in range(SAMPLES):
-            nc.scalar.dma_start(
+        def load_sample(queue, n):
+            queue.dma_start(
                 out=x_raw[:, n].rearrange("p j w -> p (j w)"),
                 in_=x[n].rearrange("(p j) h w -> p (j h w)", j=PACK),
             )
+
         nc.sync.dma_start(out=w_words[:].bitcast(I32), in_=w1_words[0].bitcast(I32))
         for q in range(4):
             nc.sync.dma_start(
                 out=w_plane[32 * q : 32 * q + 4, :].bitcast(I32),
                 in_=w1_scales[0, 4 * q : 4 * q + 4, :].bitcast(I32),
             )
+        for n in range(SAMPLES):
+            load_sample(nc.scalar if n < SAMPLES // 2 else nc.gpsimd, n)
+        for row, vec in enumerate((b1, g1, be1)):
+            nc.sync.dma_start(
+                out=vec_rows[TILES * row : TILES * (row + 1), :],
+                in_=vec.rearrange("(t p) -> t p", p=P),
+            )
+        make_identity(nc, ident[:])
 
         nc.scalar.activation(out=warm[:], in_=minus_half[:], func=ACT.Gelu)
 
@@ -101,21 +104,20 @@ def tile_axialshift_pa_s_kernel(tc, x, w1_words, w1_scales, b1, g1, be1, out):
                 in_=x_grouped[:, n].rearrange("p w j -> p (w j)"),
             )
 
-        def multiply(n):
-            for h in range(HALVES):
-                y_bank = y_pool.tile([P, 2, PIX], F32, name="y_bank")
-                y_banks[(n, h)] = y_bank
-                for i in range(2):
-                    t = 2 * h + i
-                    nc.tensor.matmul_mx(
-                        out=y_bank[:, i, :],
-                        lhsT=w_words[:, 2 * P * t : 2 * P * (t + 1)].bitcast(FP4X4),
-                        lhsT_scale=w_plane[:, P * t : P * (t + 1)],
-                        rhs=x_words[:, n, :].bitcast(FP8X4),
-                        rhs_scale=x_plane[:, n, :],
-                        start=True,
-                        stop=True,
-                    )
+        def multiply(n, h):
+            y_bank = y_pool.tile([P, 2, PIX], F32, name="y_bank")
+            y_banks[(n, h)] = y_bank
+            for i in range(2):
+                t = 2 * h + i
+                nc.tensor.matmul_mx(
+                    out=y_bank[:, i, :],
+                    lhsT=w_words[:, 2 * P * t : 2 * P * (t + 1)].bitcast(FP4X4),
+                    lhsT_scale=w_plane[:, P * t : P * (t + 1)],
+                    rhs=x_words[:, n, :].bitcast(FP8X4),
+                    rhs_scale=x_plane[:, n, :],
+                    start=True,
+                    stop=True,
+                )
 
         def channel_stats(n, h):
             nc.vector.bn_stats(
@@ -123,12 +125,16 @@ def tile_axialshift_pa_s_kernel(tc, x, w1_words, w1_scales, b1, g1, be1, out):
                 in_=y_banks[(n, h)][:].rearrange("p i w -> p w i"),
             )
 
-        def partition_sums(n):
+        def add_bias(n):
             triples = stats[:, n].rearrange("p h i s -> p (h i) s")
             nc.vector.tensor_tensor(
                 out=triples[:, :, 1:3], in0=triples[:, :, 1:3], in1=bias_eps[:], op=ALU.add
             )
+
+        def aggregate(n):
             nc.vector.bn_aggr(out=partial[:, n, 0:2], in_=stats[:, n].rearrange("p h i s -> p (h i s)"))
+
+        def partition_sums(n):
             nc.vector.scalar_tensor_tensor(
                 out=partial[:, n, 1:2],
                 in0=partial[:, n, 0:1],
@@ -199,27 +205,34 @@ def tile_axialshift_pa_s_kernel(tc, x, w1_words, w1_scales, b1, g1, be1, out):
                 out=bias_gain[:], in0=vec_cols[:, 0:TILES], in1=gain_offset[:, 0, 0:TILES], op=ALU.mult
             )
 
-        regroup(nc.vector.tensor_copy, 0)
-        for n in range(1, SAMPLES):
-            regroup(nc.scalar.copy, n)
-        quantise(0)
-        multiply(0)
-
         for n in range(SAMPLES):
-            channel_stats(n, 0)
-            if n + 1 < SAMPLES:
-                quantise(n + 1)
-                multiply(n + 1)
-            channel_stats(n, 1)
-            if n == 0:
+            regroup(nc.vector.tensor_copy if n < AHEAD else nc.scalar.copy, n)
+            if n < AHEAD:
+                quantise(n)
+        multiply(0, 0)
+        multiply(0, 1)
+
+        for i in range(SAMPLES + 2):
+            if 1 <= i < SAMPLES:
+                multiply(i, 1)
+            if i < SAMPLES:
+                channel_stats(i, 0)
+            if 1 <= i <= SAMPLES:
+                aggregate(i - 1)
+                partition_sums(i - 1)
+            if i >= 2:
+                norm_second(i - 2)
+                gelu_store(i - 2)
+            if i + AHEAD < SAMPLES:
+                quantise(i + AHEAD)
+            if i + 1 < SAMPLES:
+                multiply(i + 1, 0)
+            if i < SAMPLES:
+                channel_stats(i, 1)
+            if i == 0:
                 spread_vectors()
                 totals = small_pool.tile([P, SAMPLES, 4], F32, tag="small")
-            else:
-                norm_first(n - 1)
-            partition_sums(n)
-            if n >= 1:
-                norm_second(n - 1)
-                gelu_store(n - 1)
-        norm_first(SAMPLES - 1)
-        norm_second(SAMPLES - 1)
-        gelu_store(SAMPLES - 1)
+            if i < SAMPLES:
+                add_bias(i)
+            if 1 <= i <= SAMPLES:
+                norm_first(i - 1)

@@ -1,7 +1,6 @@
 from contextlib import ExitStack
 
 import concourse.mybir as mybir
-from concourse.masks import make_identity
 
 F32 = mybir.dt.float32
 BF16 = mybir.dt.bfloat16
@@ -20,6 +19,7 @@ CHANNELS = 512
 PIX = 256
 TILES = CHANNELS // P
 HALVES = 2
+TRIPLE = 3
 EPS = 1e-5
 Y_BANKS = 7
 AHEAD = 2
@@ -32,7 +32,7 @@ def tile_axialshift_pa_s_kernel(tc, x, w1_words, w1_scales, b1, g1, be1, out):
     with ExitStack() as ctx:
         keep = ctx.enter_context(tc.tile_pool(name="keep", bufs=1))
         y_pool = ctx.enter_context(tc.psum_pool(name="y", bufs=Y_BANKS))
-        small_pool = ctx.enter_context(tc.psum_pool(name="small", bufs=1))
+        sum_pool = ctx.enter_context(tc.psum_pool(name="sums", bufs=1))
         ctx.enter_context(tc.manual_schedule())
 
         w_words = keep.tile([P, 2 * CHANNELS], U8, align_bytes=64)
@@ -43,8 +43,9 @@ def tile_axialshift_pa_s_kernel(tc, x, w1_words, w1_scales, b1, g1, be1, out):
         x_plane = keep.tile([P, SAMPLES, PIX], U8, align_bytes=64)
         result = keep.tile([P, SAMPLES, TILES, PIX], F32)
 
-        vec_rows = keep.tile([P, P], BF16)
-        ident = keep.tile([P, P], BF16)
+        bias_col = keep.tile([P, TILES], BF16)
+        gain_col = keep.tile([P, TILES], BF16)
+        beta_col = keep.tile([P, TILES], BF16)
         mean_matrix = keep.tile([P, P], F32)
         minus_half = keep.tile([P, 1], F32)
         warm = keep.tile([P, 1], F32)
@@ -52,17 +53,17 @@ def tile_axialshift_pa_s_kernel(tc, x, w1_words, w1_scales, b1, g1, be1, out):
         bias_gain = keep.tile([P, TILES], F32)
         gain_offset = keep.tile([P, SAMPLES, 2 * TILES], F32)
         zero_beta = keep.tile([P, 2 * TILES], F32)
-        stats = keep.tile([P, SAMPLES, HALVES, 2, 3], F32)
+        stats = keep.tile([P, SAMPLES, 16], F32)
         partial = keep.tile([P, SAMPLES, 4], F32)
         var_eps = keep.tile([P, SAMPLES], F32)
         rstd = keep.tile([P, SAMPLES], F32)
         scale_shift = keep.tile([P, SAMPLES, 2 * TILES], F32)
+        totals = sum_pool.tile([P, SAMPLES, 4], F32)
 
         nc.vector.memset(w_plane[:].bitcast(I32), 0)
-        nc.vector.memset(vec_rows[:], 0.0)
+        nc.vector.memset(bias_eps[:], PIX * EPS)
         nc.vector.memset(minus_half[:], -0.5)
         nc.vector.memset(mean_matrix[:], 1.0 / P)
-        nc.vector.memset(bias_eps[:], PIX * EPS)
         nc.vector.memset(zero_beta[:], 0.0)
         nc.vector.memset(partial[:], 0.0)
 
@@ -80,14 +81,13 @@ def tile_axialshift_pa_s_kernel(tc, x, w1_words, w1_scales, b1, g1, be1, out):
             )
         for n in range(SAMPLES):
             load_sample(nc.scalar if n < SAMPLES // 2 else nc.gpsimd, n)
-        for row, vec in enumerate((b1, g1, be1)):
-            nc.sync.dma_start(
-                out=vec_rows[TILES * row : TILES * (row + 1), :],
-                in_=vec.rearrange("(t p) -> t p", p=P),
-            )
-        make_identity(nc, ident[:])
+        with nc.allow_non_contiguous_dma(reason="512 elements, one to a partition and channel tile"):
+            for col, vec in ((bias_col, b1), (gain_col, g1), (beta_col, be1)):
+                nc.sync.dma_start(out=col[:], in_=vec.rearrange("(t p) -> p t", p=P))
 
         nc.scalar.activation(out=warm[:], in_=minus_half[:], func=ACT.Gelu)
+
+        nc.gpsimd.tensor_copy(out=bias_eps[:, :, 0], in_=bias_col[:])
 
         y_banks = {}
 
@@ -121,18 +121,26 @@ def tile_axialshift_pa_s_kernel(tc, x, w1_words, w1_scales, b1, g1, be1, out):
 
         def channel_stats(n, h):
             nc.vector.bn_stats(
-                out=stats[:, n, h].rearrange("p i s -> p (i s)"),
+                out=stats[:, n, 2 * TRIPLE * h : 2 * TRIPLE * (h + 1)],
                 in_=y_banks[(n, h)][:].rearrange("p i w -> p w i"),
             )
 
         def add_bias(n):
-            triples = stats[:, n].rearrange("p h i s -> p (h i) s")
-            nc.vector.tensor_tensor(
+            triples = stats[:, n, 0 : TRIPLE * TILES].rearrange("p (t s) -> p t s", s=TRIPLE)
+            nc.gpsimd.tensor_tensor(
                 out=triples[:, :, 1:3], in0=triples[:, :, 1:3], in1=bias_eps[:], op=ALU.add
             )
 
+        def prepare_gain():
+            nc.gpsimd.tensor_copy(
+                out=gain_offset[:, :, 0:TILES],
+                in_=gain_col[:].unsqueeze(1).to_broadcast([P, SAMPLES, TILES]),
+            )
+            nc.gpsimd.tensor_tensor(out=bias_gain[:], in0=bias_col[:], in1=gain_col[:], op=ALU.mult)
+            nc.gpsimd.tensor_copy(out=zero_beta[:, TILES:], in_=beta_col[:])
+
         def aggregate(n):
-            nc.vector.bn_aggr(out=partial[:, n, 0:2], in_=stats[:, n].rearrange("p h i s -> p (h i s)"))
+            nc.vector.bn_aggr(out=partial[:, n, 0:2], in_=stats[:, n, 0 : TRIPLE * TILES])
 
         def partition_sums(n):
             nc.vector.scalar_tensor_tensor(
@@ -192,19 +200,6 @@ def tile_axialshift_pa_s_kernel(tc, x, w1_words, w1_scales, b1, g1, be1, out):
                     in_=result[:, n, t, :],
                 )
 
-        def spread_vectors():
-            vec_cols = small_pool.tile([P, P], BF16, tag="small")
-            nc.tensor.transpose(vec_cols[:], vec_rows[:], ident[:])
-            nc.vector.tensor_copy(out=bias_eps[:, :, 0], in_=vec_cols[:, 0:TILES])
-            nc.vector.tensor_copy(
-                out=gain_offset[:, :, 0:TILES],
-                in_=vec_cols[:, TILES : 2 * TILES].unsqueeze(1).to_broadcast([P, SAMPLES, TILES]),
-            )
-            nc.vector.tensor_copy(out=zero_beta[:, TILES:], in_=vec_cols[:, 2 * TILES : 3 * TILES])
-            nc.vector.tensor_tensor(
-                out=bias_gain[:], in0=vec_cols[:, 0:TILES], in1=gain_offset[:, 0, 0:TILES], op=ALU.mult
-            )
-
         for n in range(SAMPLES):
             regroup(nc.vector.tensor_copy if n < AHEAD else nc.scalar.copy, n)
             if n < AHEAD:
@@ -213,8 +208,8 @@ def tile_axialshift_pa_s_kernel(tc, x, w1_words, w1_scales, b1, g1, be1, out):
         multiply(0, 1)
 
         for i in range(SAMPLES + 2):
-            if 1 <= i < SAMPLES:
-                multiply(i, 1)
+            if i + 1 < SAMPLES:
+                multiply(i + 1, 0)
             if i < SAMPLES:
                 channel_stats(i, 0)
             if 1 <= i <= SAMPLES:
@@ -223,16 +218,15 @@ def tile_axialshift_pa_s_kernel(tc, x, w1_words, w1_scales, b1, g1, be1, out):
             if i >= 2:
                 norm_second(i - 2)
                 gelu_store(i - 2)
-            if i + AHEAD < SAMPLES:
-                quantise(i + AHEAD)
             if i + 1 < SAMPLES:
-                multiply(i + 1, 0)
+                multiply(i + 1, 1)
             if i < SAMPLES:
                 channel_stats(i, 1)
-            if i == 0:
-                spread_vectors()
-                totals = small_pool.tile([P, SAMPLES, 4], F32, tag="small")
+            if i + AHEAD < SAMPLES:
+                quantise(i + AHEAD)
             if i < SAMPLES:
                 add_bias(i)
+            if i == 0:
+                prepare_gain()
             if 1 <= i <= SAMPLES:
                 norm_first(i - 1)

@@ -42,6 +42,7 @@ def tile_axialshift_pa_s_kernel(tc, x, w1_words, w1_scales, b1, g1, be1, out):
         x_words = keep.tile([P, SAMPLES, PIX], U32, align_bytes=64)
         x_plane = keep.tile([P, SAMPLES, PIX], U8, align_bytes=64)
         result = keep.tile([P, SAMPLES, TILES, PIX], F32)
+        first_bank_copy = keep.tile([P, 2, PIX], F32)
 
         bias_col = keep.tile([P, TILES], BF16)
         gain_col = keep.tile([P, TILES], BF16)
@@ -125,6 +126,10 @@ def tile_axialshift_pa_s_kernel(tc, x, w1_words, w1_scales, b1, g1, be1, out):
                 in_=y_banks[(n, h)][:].rearrange("p i w -> p w i"),
             )
 
+        def move_to_sbuf(n, h):
+            nc.scalar.copy(out=first_bank_copy[:], in_=y_banks[(n, h)][:])
+            y_banks[(n, h)] = first_bank_copy
+
         def add_bias(n):
             triples = stats[:, n, 0 : TRIPLE * TILES].rearrange("p (t s) -> p t s", s=TRIPLE)
             nc.gpsimd.tensor_tensor(
@@ -207,26 +212,29 @@ def tile_axialshift_pa_s_kernel(tc, x, w1_words, w1_scales, b1, g1, be1, out):
         multiply(0, 0)
         multiply(0, 1)
 
-        for i in range(SAMPLES + 2):
+        for i in range(SAMPLES + 3):
             if i + 1 < SAMPLES:
                 multiply(i + 1, 0)
             if i < SAMPLES:
                 channel_stats(i, 0)
+            if i == 0:
+                move_to_sbuf(0, 0)
+            if i >= 3:
+                norm_second(i - 3)
+                gelu_store(i - 3)
             if 1 <= i <= SAMPLES:
                 aggregate(i - 1)
-                partition_sums(i - 1)
-            if i >= 2:
-                norm_second(i - 2)
-                gelu_store(i - 2)
+            if 2 <= i <= SAMPLES + 1:
+                norm_first(i - 2)
             if i + 1 < SAMPLES:
                 multiply(i + 1, 1)
             if i < SAMPLES:
                 channel_stats(i, 1)
+            if 1 <= i <= SAMPLES:
+                partition_sums(i - 1)
             if i + AHEAD < SAMPLES:
                 quantise(i + AHEAD)
             if i < SAMPLES:
                 add_bias(i)
             if i == 0:
                 prepare_gain()
-            if 1 <= i <= SAMPLES:
-                norm_first(i - 1)

@@ -81,7 +81,7 @@ def tile_axialshift_pa_s_kernel(tc, x, w1_words, w1_scales, b1, g1, be1, out):
                 in_=w1_scales[0, 4 * q : 4 * q + 4, :].bitcast(I32),
             )
         for n in range(SAMPLES):
-            load_sample(nc.scalar if n < SAMPLES // 2 else nc.gpsimd, n)
+            load_sample(nc.scalar if n < SAMPLES - 1 else nc.gpsimd, n)
         with nc.allow_non_contiguous_dma(reason="512 elements, one to a partition and channel tile"):
             for col, vec in ((bias_col, b1), (gain_col, g1), (beta_col, be1)):
                 nc.sync.dma_start(out=col[:], in_=vec.rearrange("(t p) -> p t", p=P))

@@ -74,14 +74,15 @@ def tile_axialshift_pa_s_kernel(tc, x, w1_words, w1_scales, b1, g1, be1, out):
                 in_=x[n].rearrange("(p j) h w -> p (j h w)", j=PACK),
             )
 
+        load_sample(nc.sync, 0)
         nc.sync.dma_start(out=w_words[:].bitcast(I32), in_=w1_words[0].bitcast(I32))
         for q in range(4):
             nc.sync.dma_start(
                 out=w_plane[32 * q : 32 * q + 4, :].bitcast(I32),
                 in_=w1_scales[0, 4 * q : 4 * q + 4, :].bitcast(I32),
             )
-        for n in range(SAMPLES):
-            load_sample(nc.scalar if n < SAMPLES - 1 else nc.gpsimd, n)
+        for n in range(1, SAMPLES):
+            load_sample(nc.sync if n < SAMPLES - 1 else nc.gpsimd, n)
         with nc.allow_non_contiguous_dma(reason="512 elements, one to a partition and channel tile"):
             for col, vec in ((bias_col, b1), (gain_col, g1), (beta_col, be1)):
                 nc.sync.dma_start(out=col[:], in_=vec.rearrange("(t p) -> p t", p=P))

@@ -82,7 +82,7 @@ def tile_axialshift_pa_s_kernel(tc, x, w1_words, w1_scales, b1, g1, be1, out):
                 in_=w1_scales[0, 4 * q : 4 * q + 4, :].bitcast(I32),
             )
         for n in range(1, SAMPLES):
-            load_sample(nc.sync if n < SAMPLES - 1 else nc.gpsimd, n)
+            load_sample(nc.sync, n)
         with nc.allow_non_contiguous_dma(reason="512 elements, one to a partition and channel tile"):
             for col, vec in ((bias_col, b1), (gain_col, g1), (beta_col, be1)):
                 nc.sync.dma_start(out=col[:], in_=vec.rearrange("(t p) -> p t", p=P))

@@ -93,10 +93,10 @@ def tile_axialshift_pa_s_kernel(tc, x, w1_words, w1_scales, b1, g1, be1, out):
 
         y_banks = {}
 
-        def regroup(engine_copy, n):
+        def regroup(engine_copy, n, first=0, last=PIX // 4):
             engine_copy(
-                out=x_grouped[:, n].rearrange("p (c i) j -> p c j i", i=4),
-                in_=x_raw[:, n].rearrange("p j (c i) -> p c j i", i=4),
+                out=x_grouped[:, n].rearrange("p (c i) j -> p c j i", i=4)[:, first:last],
+                in_=x_raw[:, n].rearrange("p j (c i) -> p c j i", i=4)[:, first:last],
             )
 
         def quantise(n):
@@ -207,9 +207,12 @@ def tile_axialshift_pa_s_kernel(tc, x, w1_words, w1_scales, b1, g1, be1, out):
                 )
 
         for n in range(SAMPLES):
-            regroup(nc.vector.tensor_copy if n < AHEAD else nc.scalar.copy, n)
             if n < AHEAD:
+                regroup(nc.vector.tensor_copy, n, 0, 48)
+                regroup(nc.scalar.copy, n, 48, PIX // 4)
                 quantise(n)
+            else:
+                regroup(nc.scalar.copy, n)
         multiply(0, 0)
         multiply(0, 1)
 

@@ -75,13 +75,14 @@ def tile_axialshift_pa_s_kernel(tc, x, w1_words, w1_scales, b1, g1, be1, out):
             )
 
         load_sample(nc.sync, 0)
+        load_sample(nc.sync, 1)
         nc.sync.dma_start(out=w_words[:].bitcast(I32), in_=w1_words[0].bitcast(I32))
         for q in range(4):
             nc.sync.dma_start(
                 out=w_plane[32 * q : 32 * q + 4, :].bitcast(I32),
                 in_=w1_scales[0, 4 * q : 4 * q + 4, :].bitcast(I32),
             )
-        for n in range(1, SAMPLES):
+        for n in range(2, SAMPLES):
             load_sample(nc.sync, n)
         with nc.allow_non_contiguous_dma(reason="512 elements, one to a partition and channel tile"):
             for col, vec in ((bias_col, b1), (gain_col, g1), (beta_col, be1)):

@@ -22,6 +22,7 @@ HALVES = 2
 TRIPLE = 3
 EPS = 1e-5
 Y_BANKS = 7
+WARM_MATMULS = 6
 AHEAD = 2
 
 FLOPS = 2 * SAMPLES * PIX * CHANNELS * CHANNELS
@@ -88,6 +89,12 @@ def tile_axialshift_pa_s_kernel(tc, x, w1_words, w1_scales, b1, g1, be1, out):
             for col, vec in ((bias_col, b1), (gain_col, g1), (beta_col, be1)):
                 nc.sync.dma_start(out=col[:], in_=vec.rearrange("(t p) -> p t", p=P))
 
+        warm_bank = y_pool.tile([P, 2, PIX], F32, name="y_bank")
+        for k in range(WARM_MATMULS):
+            nc.tensor.matmul(
+                out=warm_bank[:, 0, 0:P], lhsT=mean_matrix[:], rhs=mean_matrix[:], start=True, stop=True
+            )
+
         nc.scalar.activation(out=warm[:], in_=minus_half[:], func=ACT.Gelu)
 
         nc.gpsimd.tensor_copy(out=bias_eps[:, :, 0], in_=bias_col[:])
@@ -150,11 +157,11 @@ def tile_axialshift_pa_s_kernel(tc, x, w1_words, w1_scales, b1, g1, be1, out):
             nc.vector.bn_aggr(out=partial[:, n, 0:2], in_=stats[:, n, 0 : TRIPLE * TILES])
 
         def partition_sums(n):
-            nc.vector.scalar_tensor_tensor(
+            nc.vector.tensor_scalar(
                 out=partial[:, n, 1:2],
                 in0=partial[:, n, 0:1],
-                scalar=partial[:, n, 0:1],
-                in1=partial[:, n, 1:2],
+                scalar1=partial[:, n, 0:1],
+                scalar2=partial[:, n, 1:2],
                 op0=ALU.mult,
                 op1=ALU.add,
             )

@@ -22,6 +22,7 @@ HALVES = 2
 TRIPLE = 3
 EPS = 1e-5
 Y_BANKS = 7
+VECTOR_GROUPS = (36, 24)
 WARM_MATMULS = 6
 AHEAD = 2
 
@@ -63,9 +64,9 @@ def tile_axialshift_pa_s_kernel(tc, x, w1_words, w1_scales, b1, g1, be1, out):
         totals = sum_pool.tile([P, SAMPLES, 4], F32)
 
         nc.vector.memset(w_plane[:].bitcast(I32), 0)
-        nc.vector.memset(bias_eps[:], PIX * EPS)
-        nc.vector.memset(minus_half[:], -0.5)
         nc.vector.memset(mean_matrix[:], 1.0 / P)
+        nc.vector.memset(minus_half[:], -0.5)
+        nc.vector.memset(bias_eps[:], PIX * EPS)
         nc.vector.memset(zero_beta[:], 0.0)
         nc.vector.memset(partial[:], 0.0)
 
@@ -216,8 +217,8 @@ def tile_axialshift_pa_s_kernel(tc, x, w1_words, w1_scales, b1, g1, be1, out):
 
         for n in range(SAMPLES):
             if n < AHEAD:
-                regroup(nc.vector.tensor_copy, n, 0, 48)
-                regroup(nc.scalar.copy, n, 48, PIX // 4)
+                regroup(nc.vector.tensor_copy, n, 0, VECTOR_GROUPS[n])
+                regroup(nc.scalar.copy, n, VECTOR_GROUPS[n], PIX // 4)
                 quantise(n)
             else:
                 regroup(nc.scalar.copy, n)

from contextlib import ExitStack

import concourse.mybir as mybir

F32 = mybir.dt.float32
BF16 = mybir.dt.bfloat16
I32 = mybir.dt.int32
U32 = mybir.dt.uint32
U8 = mybir.dt.uint8
FP8X4 = mybir.dt.float8_e4m3fn_x4
FP4X4 = mybir.dt.float4_e2m1fn_x4
ALU = mybir.AluOpType
ACT = mybir.ActivationFunctionType

P = 128
PACK = 4
SAMPLES = 4
CHANNELS = 512
PIX = 256
TILES = CHANNELS // P
HALVES = 2
TRIPLE = 3
EPS = 1e-5
Y_BANKS = 7
VECTOR_GROUPS = (36, 24)
WARM_MATMULS = 6
AHEAD = 2

FLOPS = 2 * SAMPLES * PIX * CHANNELS * CHANNELS


def tile_axialshift_pa_s_kernel(tc, x, w1_words, w1_scales, b1, g1, be1, out):
    nc = tc.nc
    with ExitStack() as ctx:
        keep = ctx.enter_context(tc.tile_pool(name="keep", bufs=1))
        y_pool = ctx.enter_context(tc.psum_pool(name="y", bufs=Y_BANKS))
        sum_pool = ctx.enter_context(tc.psum_pool(name="sums", bufs=1))
        ctx.enter_context(tc.manual_schedule())

        w_words = keep.tile([P, 2 * CHANNELS], U8, align_bytes=64)
        w_plane = keep.tile([P, CHANNELS], U8, align_bytes=64)
        x_raw = keep.tile([P, SAMPLES, PACK, PIX], BF16)
        x_grouped = keep.tile([P, SAMPLES, PIX, PACK], BF16, align_bytes=64)
        x_words = keep.tile([P, SAMPLES, PIX], U32, align_bytes=64)
        x_plane = keep.tile([P, SAMPLES, PIX], U8, align_bytes=64)
        result = keep.tile([P, SAMPLES, TILES, PIX], F32)
        first_bank_copy = keep.tile([P, 2, PIX], F32)

        bias_col = keep.tile([P, TILES], BF16)
        gain_col = keep.tile([P, TILES], BF16)
        beta_col = keep.tile([P, TILES], BF16)
        mean_matrix = keep.tile([P, P], F32)
        minus_half = keep.tile([P, 1], F32)
        warm = keep.tile([P, 1], F32)
        bias_eps = keep.tile([P, TILES, 2], F32)
        bias_gain = keep.tile([P, TILES], F32)
        gain_offset = keep.tile([P, SAMPLES, 2 * TILES], F32)
        zero_beta = keep.tile([P, 2 * TILES], F32)
        stats = keep.tile([P, SAMPLES, 16], F32)
        partial = keep.tile([P, SAMPLES, 4], F32)
        var_eps = keep.tile([P, SAMPLES], F32)
        rstd = keep.tile([P, SAMPLES], F32)
        scale_shift = keep.tile([P, SAMPLES, 2 * TILES], F32)
        totals = sum_pool.tile([P, SAMPLES, 4], F32)

        nc.vector.memset(w_plane[:].bitcast(I32), 0)
        nc.vector.memset(mean_matrix[:], 1.0 / P)
        nc.vector.memset(minus_half[:], -0.5)
        nc.vector.memset(bias_eps[:], PIX * EPS)
        nc.vector.memset(zero_beta[:], 0.0)
        nc.vector.memset(partial[:], 0.0)

        def load_sample(queue, n):
            queue.dma_start(
                out=x_raw[:, n].rearrange("p j w -> p (j w)"),
                in_=x[n].rearrange("(p j) h w -> p (j h w)", j=PACK),
            )

        load_sample(nc.sync, 0)
        load_sample(nc.sync, 1)
        nc.sync.dma_start(out=w_words[:].bitcast(I32), in_=w1_words[0].bitcast(I32))
        for q in range(4):
            nc.sync.dma_start(
                out=w_plane[32 * q : 32 * q + 4, :].bitcast(I32),
                in_=w1_scales[0, 4 * q : 4 * q + 4, :].bitcast(I32),
            )
        for n in range(2, SAMPLES):
            load_sample(nc.sync, n)
        with nc.allow_non_contiguous_dma(reason="512 elements, one to a partition and channel tile"):
            for col, vec in ((bias_col, b1), (gain_col, g1), (beta_col, be1)):
                nc.sync.dma_start(out=col[:], in_=vec.rearrange("(t p) -> p t", p=P))

        warm_bank = y_pool.tile([P, 2, PIX], F32, name="y_bank")
        for k in range(WARM_MATMULS):
            nc.tensor.matmul(
                out=warm_bank[:, 0, 0:P], lhsT=mean_matrix[:], rhs=mean_matrix[:], start=True, stop=True
            )

        nc.scalar.activation(out=warm[:], in_=minus_half[:], func=ACT.Gelu)

        nc.gpsimd.tensor_copy(out=bias_eps[:, :, 0], in_=bias_col[:])

        y_banks = {}

        def regroup(engine_copy, n, first=0, last=PIX // 4):
            engine_copy(
                out=x_grouped[:, n].rearrange("p (c i) j -> p c j i", i=4)[:, first:last],
                in_=x_raw[:, n].rearrange("p j (c i) -> p c j i", i=4)[:, first:last],
            )

        def quantise(n):
            nc.vector.quantize_mx(
                out=x_words[:, n, :].bitcast(FP8X4),
                scales=x_plane[:, n, :],
                in_=x_grouped[:, n].rearrange("p w j -> p (w j)"),
            )

        def multiply(n, h):
            y_bank = y_pool.tile([P, 2, PIX], F32, name="y_bank")
            y_banks[(n, h)] = y_bank
            for i in range(2):
                t = 2 * h + i
                nc.tensor.matmul_mx(
                    out=y_bank[:, i, :],
                    lhsT=w_words[:, 2 * P * t : 2 * P * (t + 1)].bitcast(FP4X4),
                    lhsT_scale=w_plane[:, P * t : P * (t + 1)],
                    rhs=x_words[:, n, :].bitcast(FP8X4),
                    rhs_scale=x_plane[:, n, :],
                    start=True,
                    stop=True,
                )

        def channel_stats(n, h):
            nc.vector.bn_stats(
                out=stats[:, n, 2 * TRIPLE * h : 2 * TRIPLE * (h + 1)],
                in_=y_banks[(n, h)][:].rearrange("p i w -> p w i"),
            )

        def move_to_sbuf(n, h):
            nc.scalar.copy(out=first_bank_copy[:], in_=y_banks[(n, h)][:])
            y_banks[(n, h)] = first_bank_copy

        def add_bias(n):
            triples = stats[:, n, 0 : TRIPLE * TILES].rearrange("p (t s) -> p t s", s=TRIPLE)
            nc.gpsimd.tensor_tensor(
                out=triples[:, :, 1:3], in0=triples[:, :, 1:3], in1=bias_eps[:], op=ALU.add
            )

        def prepare_gain():
            nc.gpsimd.tensor_copy(
                out=gain_offset[:, :, 0:TILES],
                in_=gain_col[:].unsqueeze(1).to_broadcast([P, SAMPLES, TILES]),
            )
            nc.gpsimd.tensor_tensor(out=bias_gain[:], in0=bias_col[:], in1=gain_col[:], op=ALU.mult)
            nc.gpsimd.tensor_copy(out=zero_beta[:, TILES:], in_=beta_col[:])

        def aggregate(n):
            nc.vector.bn_aggr(out=partial[:, n, 0:2], in_=stats[:, n, 0 : TRIPLE * TILES])

        def partition_sums(n):
            nc.vector.tensor_scalar(
                out=partial[:, n, 1:2],
                in0=partial[:, n, 0:1],
                scalar1=partial[:, n, 0:1],
                scalar2=partial[:, n, 1:2],
                op0=ALU.mult,
                op1=ALU.add,
            )
            nc.vector.tensor_scalar(
                out=partial[:, n, 2:3], in0=partial[:, n, 0:1], scalar1=-1.0, scalar2=None, op0=ALU.mult
            )
            nc.tensor.matmul(
                out=totals[:, n, :], lhsT=mean_matrix[:], rhs=partial[:, n, :], start=True, stop=True
            )

        def norm_first(n):
            mean, square, minus_mean = (totals[:, n, c : c + 1] for c in range(3))
            nc.vector.tensor_scalar(
                out=var_eps[:, n : n + 1], in0=mean, scalar1=minus_mean, scalar2=square,
                op0=ALU.mult, op1=ALU.add,
            )
            nc.gpsimd.tensor_tensor(
                out=rstd[:, n : n + 1], in0=var_eps[:, n : n + 1], in1=minus_half[:], op=ALU.pow
            )
            nc.vector.scalar_tensor_tensor(
                out=gain_offset[:, n, TILES:],
                in0=gain_offset[:, n, 0:TILES],
                scalar=minus_mean,
                in1=bias_gain[:],
                op0=ALU.mult,
                op1=ALU.add,
            )

        def norm_second(n):
            nc.vector.scalar_tensor_tensor(
                out=scale_shift[:, n, :],
                in0=gain_offset[:, n, :],
                scalar=rstd[:, n : n + 1],
                in1=zero_beta[:],
                op0=ALU.mult,
                op1=ALU.add,
            )

        def gelu_store(n):
            for t in range(TILES):
                nc.scalar.activation(
                    out=result[:, n, t, :],
                    in_=y_banks[(n, t // 2)][:, t % 2, :],
                    func=ACT.Gelu,
                    scale=scale_shift[:, n, t : t + 1],
                    bias=scale_shift[:, n, TILES + t : TILES + t + 1],
                )
                nc.sync.dma_start(
                    out=out[n, P * t : P * (t + 1)].rearrange("o h w -> o (h w)"),
                    in_=result[:, n, t, :],
                )

        for n in range(SAMPLES):
            if n < AHEAD:
                regroup(nc.vector.tensor_copy, n, 0, VECTOR_GROUPS[n])
                regroup(nc.scalar.copy, n, VECTOR_GROUPS[n], PIX // 4)
                quantise(n)
            else:
                regroup(nc.scalar.copy, n)
        multiply(0, 0)
        multiply(0, 1)

        for i in range(SAMPLES + 3):
            if i + 1 < SAMPLES:
                multiply(i + 1, 0)
            if i < SAMPLES:
                channel_stats(i, 0)
            if i == 0:
                move_to_sbuf(0, 0)
            if i >= 3:
                norm_second(i - 3)
                gelu_store(i - 3)
            if 1 <= i <= SAMPLES:
                aggregate(i - 1)
            if 2 <= i <= SAMPLES + 1:
                norm_first(i - 2)
            if i + 1 < SAMPLES:
                multiply(i + 1, 1)
            if i < SAMPLES:
                channel_stats(i, 1)
            if 1 <= i <= SAMPLES:
                partition_sums(i - 1)
            if i + AHEAD < SAMPLES:
                quantise(i + AHEAD)
            if i < SAMPLES:
                add_bias(i)
            if i == 0:
                prepare_gain()
